import numpy as np
import ml_dtypes


def mxq(x, axis, fmt="e4m3"):
    dtype, down = {"e4m3": (ml_dtypes.float8_e4m3fn, 7), "e5m2": (ml_dtypes.float8_e5m2, 14)}[fmt]
    v = np.moveaxis(np.asarray(x, np.float32).astype(ml_dtypes.bfloat16).astype(np.float64), axis, -1)
    blocks = v.reshape(v.shape[:-1] + (-1, 32))
    amax = np.abs(blocks).max(-1, keepdims=True)
    byte = np.maximum(np.where(amax > 0, np.frexp(amax)[1] - 1 + 127, 0) - down, 1)
    scale = np.exp2(byte - 127.0)
    codes = (blocks / scale).astype(np.float32).astype(dtype).astype(np.float64)
    return np.moveaxis((codes * scale).reshape(v.shape), -1, axis)


WIDE = False


def mx_kscale(k):
    if not WIDE:
        return np.ones(k)
    levels = np.array([10, -10, 5, -5, 0])
    a = np.random.permutation(np.resize(levels, k // 512 * 4)).reshape(k // 512, 4)
    idx = np.arange(k)
    return np.exp2(a[idx // 512, idx % 128 // 32])


BF16 = ml_dtypes.bfloat16


def bf(x):
    return np.asarray(x, np.float32).astype(BF16)


def f64(x):
    return np.asarray(x).astype(np.float64)


H, D, L = 4, 1024, 512
HD = H * D


def split_heads(x):
    return x.reshape(L, H, D).transpose(1, 2, 0)


def setup_inputs():
    s, t = mx_kscale(D), mx_kscale(L)
    tr = np.repeat(t, HD // L)
    e = np.exp(1.5 * np.random.standard_normal((H, L, L)))
    return {"attn": bf(e / e.sum(0, keepdims=True) / t),
            "tokens": bf(np.random.standard_normal((D, L)) * s[:, None]),
            "Wv": bf(np.random.standard_normal((HD, D)) * 0.5 / np.sqrt(D) / s * tr[:, None]),
            "bv": bf(np.random.standard_normal(HD) * 0.15 * tr)}


def reference(attn, tokens, Wv, bv):
    v = split_heads((mxq(f64(Wv), 1, "e4m3") @ mxq(f64(tokens), 0, "e4m3")) + f64(bv)[:, None])
    return mxq(v, 2, "e4m3") @ mxq(f64(attn).transpose(0, 2, 1), 1, "e4m3")

@@ -1,0 +1,233 @@
+from contextlib import ExitStack
+
+import concourse.mybir as mybir
+from concourse.masks import make_identity
+
+F32 = mybir.dt.float32
+BF16 = mybir.dt.bfloat16
+U32 = mybir.dt.uint32
+U8 = mybir.dt.uint8
+FP8X4 = mybir.dt.float8_e4m3fn_x4
+ADD = mybir.AluOpType.add
+
+P = 128
+FLOPS = 2 * 4096 * 1024 * 512 + 2 * 4 * 1024 * 512 * 512
+
+
+def tile_selfattention_pb_kernel(tc, attn, tokens, Wv, bv, out):
+    nc = tc.nc
+    tok_v = tokens.rearrange("(g a q b) c -> g q a b c", g=2, a=2, q=P, b=2)
+    w_v = Wv.rearrange("(u p e j) k -> j u p e k", u=2, p=P, e=2, j=8)
+    attn_v = attn.rearrange("h (s p) m -> h p s m", p=P)
+    bv_v = bv.rearrange("(u p x) -> p u x", u=2, p=P, x=16)
+    out_v = out.rearrange("h (d i c) l -> h d i (c l)", d=2, i=P, c=4)
+
+    with ExitStack() as ctx:
+        keep = ctx.enter_context(tc.tile_pool(name="keep", bufs=1))
+        wraw_pool = ctx.enter_context(tc.tile_pool(name="wraw", bufs=8))
+        araw_pool = ctx.enter_context(tc.tile_pool(name="araw", bufs=4))
+        two = ctx.enter_context(tc.tile_pool(name="two", bufs=2))
+        outp = ctx.enter_context(tc.tile_pool(name="outp", bufs=3))
+        psum = ctx.enter_context(tc.psum_pool(name="psum", bufs=8))
+        ctx.enter_context(tc.manual_schedule())
+
+        braw = keep.tile([P, 32], BF16, name="braw")
+        nc.scalar.dma_start(out=braw[:].rearrange("p (u x) -> p u x", u=2), in_=bv_v)
+        traw = keep.tile([P, 4096], BF16, name="traw")
+        for g in range(2):
+            nc.sync.dma_start(
+                out=traw[:, g * 2048:(g + 1) * 2048].rearrange("q (a b c) -> q a b c", a=2, b=2),
+                in_=tok_v[g],
+            )
+        wraw = {}
+        araw = {}
+
+        def load_w(j):
+            wraw[j] = wraw_pool.tile([P, 4096], BF16, name="wraw", tag="wraw")
+            for u in range(2):
+                nc.sync.dma_start(
+                    out=wraw[j][:, u * 2048:(u + 1) * 2048].rearrange("p (e k) -> p e k", e=2),
+                    in_=w_v[j, u],
+                )
+
+        def load_a(h):
+            araw[h] = araw_pool.tile([P, 2048], BF16, name="araw", tag="araw")
+            nc.sync.dma_start(out=araw[h][:].rearrange("p (s m) -> p s m", s=4), in_=attn_v[h])
+
+        load_w(0)
+        load_a(0)
+        load_w(1)
+        load_w(2)
+        load_a(1)
+        load_w(3)
+        load_w(4)
+        load_a(2)
+        load_w(5)
+        load_w(6)
+        load_a(3)
+        load_w(7)
+
+        ident = keep.tile([P, P], F32, name="ident")
+        make_identity(nc, ident[:])
+
+        tgrp = keep.tile([P, 4096], BF16, name="tgrp", align_bytes=64)
+        tcod = keep.tile([P, 1024], U32, name="tcod", align_bytes=64)
+        tscl = keep.tile([P, 1024], U8, name="tscl", align_bytes=64)
+        for g in range(2):
+            nc.vector.tensor_copy(
+                out=tgrp[:, g * 2048:(g + 1) * 2048].rearrange("q (k i t) -> q k i t", k=4, i=P, t=4),
+                in_=traw[:, g * 2048:(g + 1) * 2048].rearrange("q (t i k) -> q k i t", t=4, i=P, k=4),
+            )
+        for g in range(2):
+            nc.vector.quantize_mx(
+                out=tcod[:, g * 512:(g + 1) * 512].bitcast(FP8X4),
+                scales=tscl[:, g * 512:(g + 1) * 512],
+                in_=tgrp[:, g * 2048:(g + 1) * 2048],
+            )
+        biasf = keep.tile([P, 32], F32, name="biasf")
+        nc.vector.tensor_copy(
+            out=biasf[:].rearrange("p (j t) -> p j t", t=4),
+            in_=braw[:].rearrange("p (t j) -> p j t", t=4),
+        )
+
+        wgrp = {}
+        wcod = {}
+        wscl = {}
+        agrp = {}
+        acod = {}
+        ascl = {}
+        vgrp = {}
+        vcod = {}
+        vscl = {}
+        osb = {}
+
+        def trans_w(j):
+            wgrp[j] = two.tile([P, 4096], BF16, name="wgrp", tag="wgrp", align_bytes=64)
+            w32 = wraw[j][:].bitcast(F32)
+            g32 = wgrp[j][:].bitcast(F32)
+            for t in range(4):
+                bank = psum.tile([P, 512], F32, name="bank", tag="bank")
+                for x in range(4):
+                    nc.tensor.transpose(
+                        bank[:, x * P:(x + 1) * P],
+                        w32[:, t * 512 + x * P:t * 512 + (x + 1) * P],
+                        ident[:],
+                    )
+                nc.scalar.copy(
+                    out=g32[:, t * 512:(t + 1) * 512].rearrange("p (g c a) -> p g c a", g=2, c=P, a=2),
+                    in_=bank[:].rearrange("p (g a c) -> p g c a", g=2, a=2, c=P),
+                )
+
+        def quant_w(j, half):
+            if half == 0:
+                wcod[j] = two.tile([P, 1024], U32, name="wcod", tag="wcod", align_bytes=64)
+                wscl[j] = two.tile([P, 1024], U8, name="wscl", tag="wscl", align_bytes=64)
+            nc.vector.quantize_mx(
+                out=wcod[j][:, half * 512:(half + 1) * 512].bitcast(FP8X4),
+                scales=wscl[j][:, half * 512:(half + 1) * 512],
+                in_=wgrp[j][:, half * 2048:(half + 1) * 2048],
+            )
+
+        def trans_a(h, half):
+            if half == 0:
+                agrp[h] = two.tile([P, 2048], BF16, name="agrp", tag="agrp", align_bytes=64)
+            a32 = araw[h][:].bitcast(F32)
+            g32 = agrp[h][:].bitcast(F32)
+            bank = psum.tile([P, 512], F32, name="bank", tag="bank")
+            for a in range(2):
+                for s in range(2):
+                    col = (2 * half + s) * 256 + a * P
+                    nc.tensor.transpose(
+                        bank[:, (2 * a + s) * P:(2 * a + s + 1) * P],
+                        a32[:, col:col + P],
+                        ident[:],
+                    )
+            nc.scalar.copy(
+                out=g32[:, half * 512:(half + 1) * 512].rearrange("p (l a) -> p l a", a=2),
+                in_=bank[:].rearrange("p (a l) -> p l a", a=2),
+            )
+
+        def quant_a(h):
+            acod[h] = two.tile([P, 512], U32, name="acod", tag="acod", align_bytes=64)
+            ascl[h] = two.tile([P, 512], U8, name="ascl", tag="ascl", align_bytes=64)
+            nc.vector.quantize_mx(out=acod[h][:].bitcast(FP8X4), scales=ascl[h][:], in_=agrp[h][:])
+
+        def stage1(j, cc):
+            if cc == 0:
+                vgrp[j] = two.tile([P, 2048], BF16, name="vgrp", tag="vgrp", align_bytes=64)
+            bank = psum.tile([P, 512], F32, name="bank", tag="bank")
+            for t in range(4):
+                for g in range(2):
+                    wc = slice(t * 256 + g * P, t * 256 + (g + 1) * P)
+                    tk = slice(g * 512 + cc * P, g * 512 + (cc + 1) * P)
+                    nc.tensor.matmul_mx(
+                        out=bank[:, t * P:(t + 1) * P],
+                        lhsT=wcod[j][:, wc].bitcast(FP8X4),
+                        lhsT_scale=wscl[j][:, wc],
+                        rhs=tcod[:, tk].bitcast(FP8X4),
+                        rhs_scale=tscl[:, tk],
+                        start=(g == 0),
+                        stop=(g == 1),
+                    )
+            nc.vector.tensor_tensor(
+                out=vgrp[j][:, cc * 512:(cc + 1) * 512].rearrange("p (c t) -> p c t", t=4),
+                in0=bank[:].rearrange("p (t c) -> p c t", t=4),
+                in1=biasf[:, j * 4:(j + 1) * 4].unsqueeze(1).to_broadcast([P, P, 4]),
+                op=ADD,
+            )
+
+        def quant_v(j):
+            vcod[j] = two.tile([P, 512], U32, name="vcod", tag="vcod", align_bytes=64)
+            vscl[j] = two.tile([P, 512], U8, name="vscl", tag="vscl", align_bytes=64)
+            nc.vector.quantize_mx(out=vcod[j][:].bitcast(FP8X4), scales=vscl[j][:], in_=vgrp[j][:])
+
+        def stage2(j, cc):
+            h = j // 2
+            if cc == 0:
+                osb[j] = outp.tile([P, 2048], F32, name="osb", tag="osb")
+            bank = psum.tile([P, 512], F32, name="bank", tag="bank")
+            vc = slice(cc * P, (cc + 1) * P)
+            nc.tensor.matmul_mx(
+                out=bank[:],
+                lhsT=vcod[j][:, vc].bitcast(FP8X4),
+                lhsT_scale=vscl[j][:, vc],
+                rhs=acod[h][:].bitcast(FP8X4),
+                rhs_scale=ascl[h][:],
+                start=True,
+                stop=True,
+            )
+            nc.scalar.copy(out=osb[j][:, cc * 512:(cc + 1) * 512], in_=bank[:])
+            if cc == 3:
+                nc.sync.dma_start(out=out_v[h, j % 2], in_=osb[j][:])
+
+        trans_w(0)
+        trans_a(0, 0)
+        trans_a(0, 1)
+        quant_w(0, 0)
+        quant_w(0, 1)
+        quant_a(0)
+        stage1(0, 0)
+        stage1(0, 1)
+        trans_w(1)
+        quant_w(1, 0)
+        stage1(0, 2)
+        quant_w(1, 1)
+        stage1(0, 3)
+
+        for i in range(8):
+            jt = i + 2
+            js = i + 1
+            if jt < 8:
+                trans_w(jt)
+                trans_a(jt // 2, jt % 2)
+            quant_v(i)
+            if jt < 8:
+                quant_w(jt, 0)
+            for cc in range(4):
+                if js < 8:
+                    stage1(js, cc)
+                if cc == 0 and jt < 8:
+                    quant_w(jt, 1)
+                if cc == 1 and jt < 8 and jt % 2 == 1:
+                    quant_a(jt // 2)
+                stage2(i, cc)

@@ -45,18 +45,23 @@ def tile_selfattention_pb_kernel(tc, attn, tokens, Wv, bv, out):
         def load_w(j):
             wraw[j] = wraw_pool.tile([P, 4096], BF16, name="wraw", tag="wraw")
             for u in range(2):
-                nc.sync.dma_start(
-                    out=wraw[j][:, u * 2048:(u + 1) * 2048].rearrange("p (e k) -> p e k", e=2),
-                    in_=w_v[j, u],
-                )
+                if j == 0:
+                    for e in range(2):
+                        t = 2 * u + e
+                        nc.sync.dma_start(out=wraw[j][:, t * 1024:(t + 1) * 1024], in_=w_v[j, u][:, e, :])
+                else:
+                    nc.sync.dma_start(
+                        out=wraw[j][:, u * 2048:(u + 1) * 2048].rearrange("p (e k) -> p e k", e=2),
+                        in_=w_v[j, u],
+                    )
 
         def load_a(h):
             araw[h] = araw_pool.tile([P, 2048], BF16, name="araw", tag="araw")
             nc.sync.dma_start(out=araw[h][:].rearrange("p (s m) -> p s m", s=4), in_=attn_v[h])
 
         load_w(0)
-        load_a(0)
         load_w(1)
+        load_a(0)
         load_w(2)
         load_a(1)
         load_w(3)
@@ -73,11 +78,17 @@ def tile_selfattention_pb_kernel(tc, attn, tokens, Wv, bv, out):
         tgrp = keep.tile([P, 4096], BF16, name="tgrp", align_bytes=64)
         tcod = keep.tile([P, 1024], U32, name="tcod", align_bytes=64)
         tscl = keep.tile([P, 1024], U8, name="tscl", align_bytes=64)
-        for g in range(2):
-            nc.vector.tensor_copy(
-                out=tgrp[:, g * 2048:(g + 1) * 2048].rearrange("q (k i t) -> q k i t", k=4, i=P, t=4),
-                in_=traw[:, g * 2048:(g + 1) * 2048].rearrange("q (t i k) -> q k i t", t=4, i=P, k=4),
+        def regroup(copy, g, k0, nk):
+            copy(
+                out=tgrp[:, g * 2048 + k0 * 512:g * 2048 + (k0 + nk) * 512].rearrange(
+                    "q (k i t) -> q k i t", k=nk, i=P, t=4),
+                in_=traw[:, g * 2048:(g + 1) * 2048].rearrange(
+                    "q (t i k) -> q k i t", t=4, i=P, k=4)[:, k0:k0 + nk],
             )
+
+        regroup(nc.vector.tensor_copy, 0, 0, 4)
+        regroup(nc.vector.tensor_copy, 1, 0, 2)
+        regroup(nc.scalar.copy, 1, 2, 2)
         for g in range(2):
             nc.vector.quantize_mx(
                 out=tcod[:, g * 512:(g + 1) * 512].bitcast(FP8X4),
@@ -118,14 +129,14 @@ def tile_selfattention_pb_kernel(tc, attn, tokens, Wv, bv, out):
                     in_=bank[:].rearrange("p (g a c) -> p g c a", g=2, a=2, c=P),
                 )
 
-        def quant_w(j, half):
-            if half == 0:
+        def quant_w(j, t0, nt):
+            if t0 == 0:
                 wcod[j] = two.tile([P, 1024], U32, name="wcod", tag="wcod", align_bytes=64)
                 wscl[j] = two.tile([P, 1024], U8, name="wscl", tag="wscl", align_bytes=64)
             nc.vector.quantize_mx(
-                out=wcod[j][:, half * 512:(half + 1) * 512].bitcast(FP8X4),
-                scales=wscl[j][:, half * 512:(half + 1) * 512],
-                in_=wgrp[j][:, half * 2048:(half + 1) * 2048],
+                out=wcod[j][:, t0 * 256:(t0 + nt) * 256].bitcast(FP8X4),
+                scales=wscl[j][:, t0 * 256:(t0 + nt) * 256],
+                in_=wgrp[j][:, t0 * 1024:(t0 + nt) * 1024],
             )
 
         def trans_a(h, half):
@@ -176,10 +187,15 @@ def tile_selfattention_pb_kernel(tc, attn, tokens, Wv, bv, out):
                 op=ADD,
             )
 
-        def quant_v(j):
-            vcod[j] = two.tile([P, 512], U32, name="vcod", tag="vcod", align_bytes=64)
-            vscl[j] = two.tile([P, 512], U8, name="vscl", tag="vscl", align_bytes=64)
-            nc.vector.quantize_mx(out=vcod[j][:].bitcast(FP8X4), scales=vscl[j][:], in_=vgrp[j][:])
+        def quant_v(j, c0, ncc):
+            if c0 == 0:
+                vcod[j] = two.tile([P, 512], U32, name="vcod", tag="vcod", align_bytes=64)
+                vscl[j] = two.tile([P, 512], U8, name="vscl", tag="vscl", align_bytes=64)
+            nc.vector.quantize_mx(
+                out=vcod[j][:, c0 * P:(c0 + ncc) * P].bitcast(FP8X4),
+                scales=vscl[j][:, c0 * P:(c0 + ncc) * P],
+                in_=vgrp[j][:, c0 * 512:(c0 + ncc) * 512],
+            )
 
         def stage2(j, cc):
             h = j // 2
@@ -197,37 +213,63 @@ def tile_selfattention_pb_kernel(tc, attn, tokens, Wv, bv, out):
                 stop=True,
             )
             nc.scalar.copy(out=osb[j][:, cc * 512:(cc + 1) * 512], in_=bank[:])
-            if cc == 3:
-                nc.sync.dma_start(out=out_v[h, j % 2], in_=osb[j][:])
+
+        def store(j, c0, ncc):
+            cols = slice(c0 * 512, (c0 + ncc) * 512)
+            nc.sync.dma_start(out=out_v[j // 2, j % 2][:, cols], in_=osb[j][:, cols])
 
         trans_w(0)
-        trans_a(0, 0)
-        trans_a(0, 1)
-        quant_w(0, 0)
-        quant_w(0, 1)
-        quant_a(0)
+        for t in range(4):
+            quant_w(0, t, 1)
         stage1(0, 0)
         stage1(0, 1)
         trans_w(1)
-        quant_w(1, 0)
+        trans_a(0, 0)
+        trans_a(0, 1)
+        quant_w(1, 0, 2)
         stage1(0, 2)
-        quant_w(1, 1)
+        quant_w(1, 2, 2)
         stage1(0, 3)
+        quant_a(0)
 
-        for i in range(8):
+        for i in range(6):
             jt = i + 2
             js = i + 1
-            if jt < 8:
-                trans_w(jt)
-                trans_a(jt // 2, jt % 2)
-            quant_v(i)
-            if jt < 8:
-                quant_w(jt, 0)
+            trans_w(jt)
+            trans_a(jt // 2, jt % 2)
+            quant_v(i, 0, 4)
+            quant_w(jt, 0, 2)
             for cc in range(4):
-                if js < 8:
-                    stage1(js, cc)
-                if cc == 0 and jt < 8:
-                    quant_w(jt, 1)
-                if cc == 1 and jt < 8 and jt % 2 == 1:
+                stage1(js, cc)
+                if cc == 0:
+                    quant_w(jt, 2, 2)
+                if cc == 1 and jt % 2 == 1:
                     quant_a(jt // 2)
+                if cc == 2 and i == 5:
+                    quant_v(js, 0, 2)
                 stage2(i, cc)
+            store(i, 0, 4)
+
+        quant_v(6, 2, 2)
+        stage1(7, 0)
+        stage2(6, 0)
+        stage1(7, 1)
+        stage2(6, 1)
+        store(6, 0, 2)
+        quant_v(7, 0, 1)
+        stage1(7, 2)
+        stage2(6, 2)
+        quant_v(7, 1, 1)
+        stage1(7, 3)
+        stage2(6, 3)
+        store(6, 2, 2)
+        quant_v(7, 2, 1)
+        stage2(7, 0)
+        store(7, 0, 1)
+        stage2(7, 1)
+        store(7, 1, 1)
+        quant_v(7, 3, 1)
+        stage2(7, 2)
+        store(7, 2, 1)
+        stage2(7, 3)
+        store(7, 3, 1)

@@ -163,29 +163,33 @@ def tile_selfattention_pb_kernel(tc, attn, tokens, Wv, bv, out):
             ascl[h] = two.tile([P, 512], U8, name="ascl", tag="ascl", align_bytes=64)
             nc.vector.quantize_mx(out=acod[h][:].bitcast(FP8X4), scales=ascl[h][:], in_=agrp[h][:])
 
-        def stage1(j, cc):
-            if cc == 0:
+        def stage1(j, c0, ncc=1):
+            if c0 == 0:
                 vgrp[j] = two.tile([P, 2048], BF16, name="vgrp", tag="vgrp", align_bytes=64)
-            bank = psum.tile([P, 512], F32, name="bank", tag="bank")
+            banks = {}
+            for cc in range(c0, c0 + ncc):
+                banks[cc] = psum.tile([P, 512], F32, name="bank", tag="bank")
             for t in range(4):
-                for g in range(2):
-                    wc = slice(t * 256 + g * P, t * 256 + (g + 1) * P)
-                    tk = slice(g * 512 + cc * P, g * 512 + (cc + 1) * P)
-                    nc.tensor.matmul_mx(
-                        out=bank[:, t * P:(t + 1) * P],
-                        lhsT=wcod[j][:, wc].bitcast(FP8X4),
-                        lhsT_scale=wscl[j][:, wc],
-                        rhs=tcod[:, tk].bitcast(FP8X4),
-                        rhs_scale=tscl[:, tk],
-                        start=(g == 0),
-                        stop=(g == 1),
-                    )
-            nc.vector.tensor_tensor(
-                out=vgrp[j][:, cc * 512:(cc + 1) * 512].rearrange("p (c t) -> p c t", t=4),
-                in0=bank[:].rearrange("p (t c) -> p c t", t=4),
-                in1=biasf[:, j * 4:(j + 1) * 4].unsqueeze(1).to_broadcast([P, P, 4]),
-                op=ADD,
-            )
+                for cc in range(c0, c0 + ncc):
+                    for g in range(2):
+                        wc = slice(t * 256 + g * P, t * 256 + (g + 1) * P)
+                        tk = slice(g * 512 + cc * P, g * 512 + (cc + 1) * P)
+                        nc.tensor.matmul_mx(
+                            out=banks[cc][:, t * P:(t + 1) * P],
+                            lhsT=wcod[j][:, wc].bitcast(FP8X4),
+                            lhsT_scale=wscl[j][:, wc],
+                            rhs=tcod[:, tk].bitcast(FP8X4),
+                            rhs_scale=tscl[:, tk],
+                            start=(g == 0),
+                            stop=(g == 1),
+                        )
+            for cc in range(c0, c0 + ncc):
+                nc.vector.tensor_tensor(
+                    out=vgrp[j][:, cc * 512:(cc + 1) * 512].rearrange("p (c t) -> p c t", t=4),
+                    in0=banks[cc][:].rearrange("p (t c) -> p c t", t=4),
+                    in1=biasf[:, j * 4:(j + 1) * 4].unsqueeze(1).to_broadcast([P, P, 4]),
+                    op=ADD,
+                )
 
         def quant_v(j, c0, ncc):
             if c0 == 0:
@@ -212,7 +216,10 @@ def tile_selfattention_pb_kernel(tc, attn, tokens, Wv, bv, out):
                 start=True,
                 stop=True,
             )
-            nc.scalar.copy(out=osb[j][:, cc * 512:(cc + 1) * 512], in_=bank[:])
+            if cc == 2 and j < 6:
+                nc.vector.tensor_copy(out=osb[j][:, cc * 512:(cc + 1) * 512], in_=bank[:])
+            else:
+                nc.scalar.copy(out=osb[j][:, cc * 512:(cc + 1) * 512], in_=bank[:])
 
         def store(j, c0, ncc):
             cols = slice(c0 * 512, (c0 + ncc) * 512)
@@ -221,15 +228,13 @@ def tile_selfattention_pb_kernel(tc, attn, tokens, Wv, bv, out):
         trans_w(0)
         for t in range(4):
             quant_w(0, t, 1)
-        stage1(0, 0)
-        stage1(0, 1)
+        stage1(0, 0, 3)
         trans_w(1)
         trans_a(0, 0)
         trans_a(0, 1)
         quant_w(1, 0, 2)
-        stage1(0, 2)
-        quant_w(1, 2, 2)
         stage1(0, 3)
+        quant_w(1, 2, 2)
         quant_a(0)
 
         for i in range(6):

@@ -18,7 +18,7 @@ def tile_selfattention_pb_kernel(tc, attn, tokens, Wv, bv, out):
     nc = tc.nc
     tok_v = tokens.rearrange("(g a q b) c -> g q a b c", g=2, a=2, q=P, b=2)
     w_v = Wv.rearrange("(u p e j) k -> j u p e k", u=2, p=P, e=2, j=8)
-    attn_v = attn.rearrange("h (s p) m -> h p s m", p=P)
+    attn_v = attn.rearrange("h (p s) m -> h p (s m)", s=4)
     bv_v = bv.rearrange("(u p x) -> p u x", u=2, p=P, x=16)
     out_v = out.rearrange("h (d i c) l -> h d i (c l)", d=2, i=P, c=4)
 
@@ -57,20 +57,20 @@ def tile_selfattention_pb_kernel(tc, attn, tokens, Wv, bv, out):
 
         def load_a(h):
             araw[h] = araw_pool.tile([P, 2048], BF16, name="araw", tag="araw")
-            nc.sync.dma_start(out=araw[h][:].rearrange("p (s m) -> p s m", s=4), in_=attn_v[h])
+            nc.sync.dma_start(out=araw[h][:], in_=attn_v[h])
 
         load_w(0)
         load_w(1)
         load_a(0)
         load_w(2)
-        load_a(1)
         load_w(3)
+        load_a(1)
         load_w(4)
-        load_a(2)
         load_w(5)
+        load_a(2)
         load_w(6)
-        load_a(3)
         load_w(7)
+        load_a(3)
 
         ident = keep.tile([P, P], F32, name="ident")
         make_identity(nc, ident[:])
@@ -145,17 +145,17 @@ def tile_selfattention_pb_kernel(tc, attn, tokens, Wv, bv, out):
             a32 = araw[h][:].bitcast(F32)
             g32 = agrp[h][:].bitcast(F32)
             bank = psum.tile([P, 512], F32, name="bank", tag="bank")
-            for a in range(2):
-                for s in range(2):
+            for s in range(2):
+                for a in range(2):
                     col = (2 * half + s) * 256 + a * P
                     nc.tensor.transpose(
-                        bank[:, (2 * a + s) * P:(2 * a + s + 1) * P],
+                        bank[:, (2 * s + a) * P:(2 * s + a + 1) * P],
                         a32[:, col:col + P],
                         ident[:],
                     )
             nc.scalar.copy(
-                out=g32[:, half * 512:(half + 1) * 512].rearrange("p (l a) -> p l a", a=2),
-                in_=bank[:].rearrange("p (a l) -> p l a", a=2),
+                out=g32.rearrange("q (p y x) -> q p y x", p=P, y=2, x=4)[:, :, half, :],
+                in_=bank[:].rearrange("q (x p) -> q p x", x=4),
             )
 
         def quant_a(h):
@@ -216,10 +216,7 @@ def tile_selfattention_pb_kernel(tc, attn, tokens, Wv, bv, out):
                 start=True,
                 stop=True,
             )
-            if cc == 2 and j < 6:
-                nc.vector.tensor_copy(out=osb[j][:, cc * 512:(cc + 1) * 512], in_=bank[:])
-            else:
-                nc.scalar.copy(out=osb[j][:, cc * 512:(cc + 1) * 512], in_=bank[:])
+            nc.scalar.copy(out=osb[j][:, cc * 512:(cc + 1) * 512], in_=bank[:])
 
         def store(j, c0, ncc):
             cols = slice(c0 * 512, (c0 + ncc) * 512)
@@ -241,33 +238,45 @@ def tile_selfattention_pb_kernel(tc, attn, tokens, Wv, bv, out):
             jt = i + 2
             js = i + 1
             trans_w(jt)
-            trans_a(jt // 2, jt % 2)
-            quant_v(i, 0, 4)
+            if jt % 2 == 1:
+                trans_a(jt // 2, 0)
+                trans_a(jt // 2, 1)
+            if i == 0:
+                quant_v(0, 0, 4)
             quant_w(jt, 0, 2)
             for cc in range(4):
                 stage1(js, cc)
-                if cc == 0:
+                if cc == 0 and i == 5:
                     quant_w(jt, 2, 2)
                 if cc == 1 and jt % 2 == 1:
                     quant_a(jt // 2)
-                if cc == 2 and i == 5:
+                if cc == 2:
                     quant_v(js, 0, 2)
                 stage2(i, cc)
-            store(i, 0, 4)
+                if cc == 1 and i == 5:
+                    store(i, 0, 2)
+            if i < 5:
+                quant_w(jt, 2, 2)
+                quant_v(js, 2, 2)
+                store(i, 0, 4)
+            else:
+                store(i, 2, 2)
 
-        quant_v(6, 2, 2)
         stage1(7, 0)
+        quant_v(6, 2, 2)
         stage2(6, 0)
+        store(6, 0, 1)
         stage1(7, 1)
         stage2(6, 1)
-        store(6, 0, 2)
+        store(6, 1, 1)
         quant_v(7, 0, 1)
         stage1(7, 2)
         stage2(6, 2)
+        store(6, 2, 1)
         quant_v(7, 1, 1)
         stage1(7, 3)
         stage2(6, 3)
-        store(6, 2, 2)
+        store(6, 3, 1)
         quant_v(7, 2, 1)
         stage2(7, 0)
         store(7, 0, 1)

@@ -18,16 +18,18 @@ def tile_selfattention_pb_kernel(tc, attn, tokens, Wv, bv, out):
     nc = tc.nc
     tok_v = tokens.rearrange("(g a q b) c -> g q a b c", g=2, a=2, q=P, b=2)
     w_v = Wv.rearrange("(u p e j) k -> j u p e k", u=2, p=P, e=2, j=8)
+    wpair_v = Wv.rearrange("(u p e h d) k -> h u p e (d k)", u=2, p=P, e=2, h=4, d=2)
     attn_v = attn.rearrange("h (p s) m -> h p (s m)", s=4)
     bv_v = bv.rearrange("(u p x) -> p u x", u=2, p=P, x=16)
     out_v = out.rearrange("h (d i c) l -> h d i (c l)", d=2, i=P, c=4)
 
     with ExitStack() as ctx:
         keep = ctx.enter_context(tc.tile_pool(name="keep", bufs=1))
-        wraw_pool = ctx.enter_context(tc.tile_pool(name="wraw", bufs=8))
+        wraw_pool = ctx.enter_context(tc.tile_pool(name="wraw", bufs=4))
+        wpair_pool = ctx.enter_context(tc.tile_pool(name="wpair", bufs=2))
         araw_pool = ctx.enter_context(tc.tile_pool(name="araw", bufs=4))
         two = ctx.enter_context(tc.tile_pool(name="two", bufs=2))
-        outp = ctx.enter_context(tc.tile_pool(name="outp", bufs=3))
+        outp = ctx.enter_context(tc.tile_pool(name="outp", bufs=4))
         psum = ctx.enter_context(tc.psum_pool(name="psum", bufs=8))
         ctx.enter_context(tc.manual_schedule())
 
@@ -42,16 +44,28 @@ def tile_selfattention_pb_kernel(tc, attn, tokens, Wv, bv, out):
         wraw = {}
         araw = {}
 
+        def load_w_pair(h):
+            pair = wpair_pool.tile([P, 8192], BF16, name="wpair", tag="wpair")
+            for u in range(2):
+                nc.sync.dma_start(
+                    out=pair[:, u * 4096:(u + 1) * 4096].rearrange("p (e x) -> p e x", e=2),
+                    in_=wpair_v[h, u],
+                )
+            words = pair[:].bitcast(F32).rearrange("p (t d w) -> p t d w", t=4, d=2)
+            for d in range(2):
+                wraw[2 * h + d] = words[:, :, d, :]
+
         def load_w(j):
-            wraw[j] = wraw_pool.tile([P, 4096], BF16, name="wraw", tag="wraw")
+            single = wraw_pool.tile([P, 4096], BF16, name="wraw", tag="wraw")
+            wraw[j] = single[:].bitcast(F32).rearrange("p (t w) -> p t w", t=4)
             for u in range(2):
                 if j == 0:
                     for e in range(2):
                         t = 2 * u + e
-                        nc.sync.dma_start(out=wraw[j][:, t * 1024:(t + 1) * 1024], in_=w_v[j, u][:, e, :])
+                        nc.sync.dma_start(out=single[:, t * 1024:(t + 1) * 1024], in_=w_v[j, u][:, e, :])
                 else:
                     nc.sync.dma_start(
-                        out=wraw[j][:, u * 2048:(u + 1) * 2048].rearrange("p (e k) -> p e k", e=2),
+                        out=single[:, u * 2048:(u + 1) * 2048].rearrange("p (e k) -> p e k", e=2),
                         in_=w_v[j, u],
                     )
 
@@ -65,11 +79,9 @@ def tile_selfattention_pb_kernel(tc, attn, tokens, Wv, bv, out):
         load_w(2)
         load_w(3)
         load_a(1)
-        load_w(4)
-        load_w(5)
+        load_w_pair(2)
         load_a(2)
-        load_w(6)
-        load_w(7)
+        load_w_pair(3)
         load_a(3)
 
         ident = keep.tile([P, P], F32, name="ident")
@@ -114,14 +126,13 @@ def tile_selfattention_pb_kernel(tc, attn, tokens, Wv, bv, out):
 
         def trans_w(j):
             wgrp[j] = two.tile([P, 4096], BF16, name="wgrp", tag="wgrp", align_bytes=64)
-            w32 = wraw[j][:].bitcast(F32)
             g32 = wgrp[j][:].bitcast(F32)
             for t in range(4):
                 bank = psum.tile([P, 512], F32, name="bank", tag="bank")
                 for x in range(4):
                     nc.tensor.transpose(
                         bank[:, x * P:(x + 1) * P],
-                        w32[:, t * 512 + x * P:t * 512 + (x + 1) * P],
+                        wraw[j][:, t, x * P:(x + 1) * P],
                         ident[:],
                     )
                 nc.scalar.copy(

@@ -18,20 +18,17 @@ def tile_selfattention_pb_kernel(tc, attn, tokens, Wv, bv, out):
     nc = tc.nc
     tok_v = tokens.rearrange("(g a q b) c -> g q a b c", g=2, a=2, q=P, b=2)
     w_v = Wv.rearrange("(u p e j) k -> j u p e k", u=2, p=P, e=2, j=8)
-    wpair_v = Wv.rearrange("(u p e h d) k -> h u p e (d k)", u=2, p=P, e=2, h=4, d=2)
     attn_v = attn.rearrange("h (p s) m -> h p (s m)", s=4)
     bv_v = bv.rearrange("(u p x) -> p u x", u=2, p=P, x=16)
     out_v = out.rearrange("h (d i c) l -> h d i (c l)", d=2, i=P, c=4)
 
     with ExitStack() as ctx:
         keep = ctx.enter_context(tc.tile_pool(name="keep", bufs=1))
-        wraw_pool = ctx.enter_context(tc.tile_pool(name="wraw", bufs=4))
-        wpair_pool = ctx.enter_context(tc.tile_pool(name="wpair", bufs=2))
+        wraw_pool = ctx.enter_context(tc.tile_pool(name="wraw", bufs=8))
         araw_pool = ctx.enter_context(tc.tile_pool(name="araw", bufs=4))
         two = ctx.enter_context(tc.tile_pool(name="two", bufs=2))
-        outp = ctx.enter_context(tc.tile_pool(name="outp", bufs=4))
+        outp = ctx.enter_context(tc.tile_pool(name="outp", bufs=3))
         psum = ctx.enter_context(tc.psum_pool(name="psum", bufs=8))
-        ctx.enter_context(tc.manual_schedule())
 
         braw = keep.tile([P, 32], BF16, name="braw")
         nc.scalar.dma_start(out=braw[:].rearrange("p (u x) -> p u x", u=2), in_=bv_v)
@@ -44,28 +41,16 @@ def tile_selfattention_pb_kernel(tc, attn, tokens, Wv, bv, out):
         wraw = {}
         araw = {}
 
-        def load_w_pair(h):
-            pair = wpair_pool.tile([P, 8192], BF16, name="wpair", tag="wpair")
-            for u in range(2):
-                nc.sync.dma_start(
-                    out=pair[:, u * 4096:(u + 1) * 4096].rearrange("p (e x) -> p e x", e=2),
-                    in_=wpair_v[h, u],
-                )
-            words = pair[:].bitcast(F32).rearrange("p (t d w) -> p t d w", t=4, d=2)
-            for d in range(2):
-                wraw[2 * h + d] = words[:, :, d, :]
-
         def load_w(j):
-            single = wraw_pool.tile([P, 4096], BF16, name="wraw", tag="wraw")
-            wraw[j] = single[:].bitcast(F32).rearrange("p (t w) -> p t w", t=4)
+            wraw[j] = wraw_pool.tile([P, 4096], BF16, name="wraw", tag="wraw")
             for u in range(2):
                 if j == 0:
                     for e in range(2):
                         t = 2 * u + e
-                        nc.sync.dma_start(out=single[:, t * 1024:(t + 1) * 1024], in_=w_v[j, u][:, e, :])
+                        nc.sync.dma_start(out=wraw[j][:, t * 1024:(t + 1) * 1024], in_=w_v[j, u][:, e, :])
                 else:
                     nc.sync.dma_start(
-                        out=single[:, u * 2048:(u + 1) * 2048].rearrange("p (e k) -> p e k", e=2),
+                        out=wraw[j][:, u * 2048:(u + 1) * 2048].rearrange("p (e k) -> p e k", e=2),
                         in_=w_v[j, u],
                     )
 
@@ -79,9 +64,11 @@ def tile_selfattention_pb_kernel(tc, attn, tokens, Wv, bv, out):
         load_w(2)
         load_w(3)
         load_a(1)
-        load_w_pair(2)
+        load_w(4)
+        load_w(5)
         load_a(2)
-        load_w_pair(3)
+        load_w(6)
+        load_w(7)
         load_a(3)
 
         ident = keep.tile([P, P], F32, name="ident")
@@ -126,13 +113,14 @@ def tile_selfattention_pb_kernel(tc, attn, tokens, Wv, bv, out):
 
         def trans_w(j):
             wgrp[j] = two.tile([P, 4096], BF16, name="wgrp", tag="wgrp", align_bytes=64)
+            w32 = wraw[j][:].bitcast(F32)
             g32 = wgrp[j][:].bitcast(F32)
             for t in range(4):
                 bank = psum.tile([P, 512], F32, name="bank", tag="bank")
                 for x in range(4):
                     nc.tensor.transpose(
                         bank[:, x * P:(x + 1) * P],
-                        wraw[j][:, t, x * P:(x + 1) * P],
+                        w32[:, t * 512 + x * P:t * 512 + (x + 1) * P],
                         ident[:],
                     )
                 nc.scalar.copy(

from contextlib import ExitStack

import concourse.mybir as mybir
from concourse.masks import make_identity

F32 = mybir.dt.float32
BF16 = mybir.dt.bfloat16
U32 = mybir.dt.uint32
U8 = mybir.dt.uint8
FP8X4 = mybir.dt.float8_e4m3fn_x4
ADD = mybir.AluOpType.add

P = 128
FLOPS = 2 * 4096 * 1024 * 512 + 2 * 4 * 1024 * 512 * 512


def tile_selfattention_pb_kernel(tc, attn, tokens, Wv, bv, out):
    nc = tc.nc
    tok_v = tokens.rearrange("(g a q b) c -> g q a b c", g=2, a=2, q=P, b=2)
    w_v = Wv.rearrange("(u p e j) k -> j u p e k", u=2, p=P, e=2, j=8)
    attn_v = attn.rearrange("h (p s) m -> h p (s m)", s=4)
    bv_v = bv.rearrange("(u p x) -> p u x", u=2, p=P, x=16)
    out_v = out.rearrange("h (d i c) l -> h d i (c l)", d=2, i=P, c=4)

    with ExitStack() as ctx:
        keep = ctx.enter_context(tc.tile_pool(name="keep", bufs=1))
        wraw_pool = ctx.enter_context(tc.tile_pool(name="wraw", bufs=8))
        araw_pool = ctx.enter_context(tc.tile_pool(name="araw", bufs=4))
        two = ctx.enter_context(tc.tile_pool(name="two", bufs=2))
        outp = ctx.enter_context(tc.tile_pool(name="outp", bufs=3))
        psum = ctx.enter_context(tc.psum_pool(name="psum", bufs=8))

        braw = keep.tile([P, 32], BF16, name="braw")
        nc.scalar.dma_start(out=braw[:].rearrange("p (u x) -> p u x", u=2), in_=bv_v)
        traw = keep.tile([P, 4096], BF16, name="traw")
        for g in range(2):
            nc.sync.dma_start(
                out=traw[:, g * 2048:(g + 1) * 2048].rearrange("q (a b c) -> q a b c", a=2, b=2),
                in_=tok_v[g],
            )
        wraw = {}
        araw = {}

        def load_w(j):
            wraw[j] = wraw_pool.tile([P, 4096], BF16, name="wraw", tag="wraw")
            for u in range(2):
                if j == 0:
                    for e in range(2):
                        t = 2 * u + e
                        nc.sync.dma_start(out=wraw[j][:, t * 1024:(t + 1) * 1024], in_=w_v[j, u][:, e, :])
                else:
                    nc.sync.dma_start(
                        out=wraw[j][:, u * 2048:(u + 1) * 2048].rearrange("p (e k) -> p e k", e=2),
                        in_=w_v[j, u],
                    )

        def load_a(h):
            araw[h] = araw_pool.tile([P, 2048], BF16, name="araw", tag="araw")
            nc.sync.dma_start(out=araw[h][:], in_=attn_v[h])

        load_w(0)
        load_w(1)
        load_a(0)
        load_w(2)
        load_w(3)
        load_a(1)
        load_w(4)
        load_w(5)
        load_a(2)
        load_w(6)
        load_w(7)
        load_a(3)

        ident = keep.tile([P, P], F32, name="ident")
        make_identity(nc, ident[:])

        tgrp = keep.tile([P, 4096], BF16, name="tgrp", align_bytes=64)
        tcod = keep.tile([P, 1024], U32, name="tcod", align_bytes=64)
        tscl = keep.tile([P, 1024], U8, name="tscl", align_bytes=64)
        def regroup(copy, g, k0, nk):
            copy(
                out=tgrp[:, g * 2048 + k0 * 512:g * 2048 + (k0 + nk) * 512].rearrange(
                    "q (k i t) -> q k i t", k=nk, i=P, t=4),
                in_=traw[:, g * 2048:(g + 1) * 2048].rearrange(
                    "q (t i k) -> q k i t", t=4, i=P, k=4)[:, k0:k0 + nk],
            )

        regroup(nc.vector.tensor_copy, 0, 0, 4)
        regroup(nc.vector.tensor_copy, 1, 0, 2)
        regroup(nc.scalar.copy, 1, 2, 2)
        for g in range(2):
            nc.vector.quantize_mx(
                out=tcod[:, g * 512:(g + 1) * 512].bitcast(FP8X4),
                scales=tscl[:, g * 512:(g + 1) * 512],
                in_=tgrp[:, g * 2048:(g + 1) * 2048],
            )
        biasf = keep.tile([P, 32], F32, name="biasf")
        nc.vector.tensor_copy(
            out=biasf[:].rearrange("p (j t) -> p j t", t=4),
            in_=braw[:].rearrange("p (t j) -> p j t", t=4),
        )

        wgrp = {}
        wcod = {}
        wscl = {}
        agrp = {}
        acod = {}
        ascl = {}
        vgrp = {}
        vcod = {}
        vscl = {}
        osb = {}

        def trans_w(j):
            wgrp[j] = two.tile([P, 4096], BF16, name="wgrp", tag="wgrp", align_bytes=64)
            w32 = wraw[j][:].bitcast(F32)
            g32 = wgrp[j][:].bitcast(F32)
            for t in range(4):
                bank = psum.tile([P, 512], F32, name="bank", tag="bank")
                for x in range(4):
                    nc.tensor.transpose(
                        bank[:, x * P:(x + 1) * P],
                        w32[:, t * 512 + x * P:t * 512 + (x + 1) * P],
                        ident[:],
                    )
                nc.scalar.copy(
                    out=g32[:, t * 512:(t + 1) * 512].rearrange("p (g c a) -> p g c a", g=2, c=P, a=2),
                    in_=bank[:].rearrange("p (g a c) -> p g c a", g=2, a=2, c=P),
                )

        def quant_w(j, t0, nt):
            if t0 == 0:
                wcod[j] = two.tile([P, 1024], U32, name="wcod", tag="wcod", align_bytes=64)
                wscl[j] = two.tile([P, 1024], U8, name="wscl", tag="wscl", align_bytes=64)
            nc.vector.quantize_mx(
                out=wcod[j][:, t0 * 256:(t0 + nt) * 256].bitcast(FP8X4),
                scales=wscl[j][:, t0 * 256:(t0 + nt) * 256],
                in_=wgrp[j][:, t0 * 1024:(t0 + nt) * 1024],
            )

        def trans_a(h, half):
            if half == 0:
                agrp[h] = two.tile([P, 2048], BF16, name="agrp", tag="agrp", align_bytes=64)
            a32 = araw[h][:].bitcast(F32)
            g32 = agrp[h][:].bitcast(F32)
            bank = psum.tile([P, 512], F32, name="bank", tag="bank")
            for s in range(2):
                for a in range(2):
                    col = (2 * half + s) * 256 + a * P
                    nc.tensor.transpose(
                        bank[:, (2 * s + a) * P:(2 * s + a + 1) * P],
                        a32[:, col:col + P],
                        ident[:],
                    )
            nc.scalar.copy(
                out=g32.rearrange("q (p y x) -> q p y x", p=P, y=2, x=4)[:, :, half, :],
                in_=bank[:].rearrange("q (x p) -> q p x", x=4),
            )

        def quant_a(h):
            acod[h] = two.tile([P, 512], U32, name="acod", tag="acod", align_bytes=64)
            ascl[h] = two.tile([P, 512], U8, name="ascl", tag="ascl", align_bytes=64)
            nc.vector.quantize_mx(out=acod[h][:].bitcast(FP8X4), scales=ascl[h][:], in_=agrp[h][:])

        def stage1(j, c0, ncc=1):
            if c0 == 0:
                vgrp[j] = two.tile([P, 2048], BF16, name="vgrp", tag="vgrp", align_bytes=64)
            banks = {}
            for cc in range(c0, c0 + ncc):
                banks[cc] = psum.tile([P, 512], F32, name="bank", tag="bank")
            for t in range(4):
                for cc in range(c0, c0 + ncc):
                    for g in range(2):
                        wc = slice(t * 256 + g * P, t * 256 + (g + 1) * P)
                        tk = slice(g * 512 + cc * P, g * 512 + (cc + 1) * P)
                        nc.tensor.matmul_mx(
                            out=banks[cc][:, t * P:(t + 1) * P],
                            lhsT=wcod[j][:, wc].bitcast(FP8X4),
                            lhsT_scale=wscl[j][:, wc],
                            rhs=tcod[:, tk].bitcast(FP8X4),
                            rhs_scale=tscl[:, tk],
                            start=(g == 0),
                            stop=(g == 1),
                        )
            for cc in range(c0, c0 + ncc):
                nc.vector.tensor_tensor(
                    out=vgrp[j][:, cc * 512:(cc + 1) * 512].rearrange("p (c t) -> p c t", t=4),
                    in0=banks[cc][:].rearrange("p (t c) -> p c t", t=4),
                    in1=biasf[:, j * 4:(j + 1) * 4].unsqueeze(1).to_broadcast([P, P, 4]),
                    op=ADD,
                )

        def quant_v(j, c0, ncc):
            if c0 == 0:
                vcod[j] = two.tile([P, 512], U32, name="vcod", tag="vcod", align_bytes=64)
                vscl[j] = two.tile([P, 512], U8, name="vscl", tag="vscl", align_bytes=64)
            nc.vector.quantize_mx(
                out=vcod[j][:, c0 * P:(c0 + ncc) * P].bitcast(FP8X4),
                scales=vscl[j][:, c0 * P:(c0 + ncc) * P],
                in_=vgrp[j][:, c0 * 512:(c0 + ncc) * 512],
            )

        def stage2(j, cc):
            h = j // 2
            if cc == 0:
                osb[j] = outp.tile([P, 2048], F32, name="osb", tag="osb")
            bank = psum.tile([P, 512], F32, name="bank", tag="bank")
            vc = slice(cc * P, (cc + 1) * P)
            nc.tensor.matmul_mx(
                out=bank[:],
                lhsT=vcod[j][:, vc].bitcast(FP8X4),
                lhsT_scale=vscl[j][:, vc],
                rhs=acod[h][:].bitcast(FP8X4),
                rhs_scale=ascl[h][:],
                start=True,
                stop=True,
            )
            nc.scalar.copy(out=osb[j][:, cc * 512:(cc + 1) * 512], in_=bank[:])

        def store(j, c0, ncc):
            cols = slice(c0 * 512, (c0 + ncc) * 512)
            nc.sync.dma_start(out=out_v[j // 2, j % 2][:, cols], in_=osb[j][:, cols])

        trans_w(0)
        for t in range(4):
            quant_w(0, t, 1)
        stage1(0, 0, 3)
        trans_w(1)
        trans_a(0, 0)
        trans_a(0, 1)
        quant_w(1, 0, 2)
        stage1(0, 3)
        quant_w(1, 2, 2)
        quant_a(0)

        for i in range(6):
            jt = i + 2
            js = i + 1
            trans_w(jt)
            if jt % 2 == 1:
                trans_a(jt // 2, 0)
                trans_a(jt // 2, 1)
            if i == 0:
                quant_v(0, 0, 4)
            quant_w(jt, 0, 2)
            for cc in range(4):
                stage1(js, cc)
                if cc == 0 and i == 5:
                    quant_w(jt, 2, 2)
                if cc == 1 and jt % 2 == 1:
                    quant_a(jt // 2)
                if cc == 2:
                    quant_v(js, 0, 2)
                stage2(i, cc)
                if cc == 1 and i == 5:
                    store(i, 0, 2)
            if i < 5:
                quant_w(jt, 2, 2)
                quant_v(js, 2, 2)
                store(i, 0, 4)
            else:
                store(i, 2, 2)

        stage1(7, 0)
        quant_v(6, 2, 2)
        stage2(6, 0)
        store(6, 0, 1)
        stage1(7, 1)
        stage2(6, 1)
        store(6, 1, 1)
        quant_v(7, 0, 1)
        stage1(7, 2)
        stage2(6, 2)
        store(6, 2, 1)
        quant_v(7, 1, 1)
        stage1(7, 3)
        stage2(6, 3)
        store(6, 3, 1)
        quant_v(7, 2, 1)
        stage2(7, 0)
        store(7, 0, 1)
        stage2(7, 1)
        store(7, 1, 1)
        quant_v(7, 3, 1)
        stage2(7, 2)
        store(7, 2, 1)
        stage2(7, 3)
        store(7, 3, 1)
